import numpy as np
import ml_dtypes


def mxq(x, axis, fmt="e4m3"):
    dtype, down = {"e4m3": (ml_dtypes.float8_e4m3fn, 7), "e5m2": (ml_dtypes.float8_e5m2, 14)}[fmt]
    v = np.moveaxis(np.asarray(x, np.float32).astype(ml_dtypes.bfloat16).astype(np.float64), axis, -1)
    blocks = v.reshape(v.shape[:-1] + (-1, 32))
    amax = np.abs(blocks).max(-1, keepdims=True)
    byte = np.maximum(np.where(amax > 0, np.frexp(amax)[1] - 1 + 127, 0) - down, 1)
    scale = np.exp2(byte - 127.0)
    codes = (blocks / scale).astype(np.float32).astype(dtype).astype(np.float64)
    return np.moveaxis((codes * scale).reshape(v.shape), -1, axis)


WIDE = False


def mx_kscale(k):
    if not WIDE:
        return np.ones(k)
    levels = np.array([10, -10, 5, -5, 0])
    if k % 512:
        return np.exp2(np.random.permutation(np.resize(levels, k // 32))).repeat(32)
    a = np.empty((k // 512, 16))
    for p in range(k // 512):
        a[p, :8] = np.random.permutation(np.resize(levels, 8))
        for g in range(8):
            far = levels[np.abs(levels - a[p, g]) >= 10]
            a[p, g + 8] = far[np.random.randint(len(far))]
    return np.exp2(a.ravel()).repeat(32)


BF16 = ml_dtypes.bfloat16


def bf(x):
    return np.asarray(x, np.float32).astype(BF16)


def f64(x):
    return np.asarray(x).astype(np.float64)


B, D0, D1, D2, D3 = 512, 2048, 2048, 2048, 2048
HEBB = 0.01
RATE = 0.001
BATCH_NUM = 1
C = HEBB * RATE / BATCH_NUM


def centred(s):
    return s / np.exp2(np.round(np.log2(s.mean())))


def draw0():
    s = centred(mx_kscale(D2))
    return {"vi": bf(np.maximum(3.0 + 5.0 * np.random.standard_normal((B, D2)), 0.0) * s),
            "W": bf(np.random.standard_normal((D3, D2)) * 0.9 / np.sqrt(D2) / s[None, :]),
            "b": bf(3.0 + 1.5 * np.random.standard_normal(D3))}


def core(vi, W, b):
    vi = f64(vi)
    vj = np.maximum((mxq(vi, 1, "e4m3") @ mxq(f64(W), 1, "e4m3").T) + f64(b), 0.0)
    m = np.mean(vj, axis=0)
    out = vj + np.sum(vi, axis=1, keepdims=True) * (C * m)[None, :]
    return out, m


def e4m3fn_bytes(y):
    return np.clip(np.asarray(y, np.float64), -448.0, 448.0).astype(np.float32).astype(ml_dtypes.float8_e4m3fn).view(np.uint8)


def e4m3fn_values(b):
    return np.asarray(b, np.uint8).view(ml_dtypes.float8_e4m3fn).astype(np.float64)


def setup_inputs():
    d = draw0()
    x0 = np.asarray(d['W']).astype(np.float64)
    s = (np.max(np.abs(x0), axis=(0,), keepdims=True) / 448.0).astype(np.float32)
    out = {}
    for k, v in d.items():
        if k == 'W':
            out['W_bytes'] = e4m3fn_bytes(x0 / s.astype(np.float64))
            out['W_scale'] = s
        else:
            out[k] = v
    return out


def reference(vi, W_bytes, W_scale, b):
    return core(vi, e4m3fn_values(W_bytes) * W_scale.astype(np.float64), b)

@@ -1,0 +1,249 @@
+from contextlib import ExitStack
+
+import concourse.mybir as mybir
+from concourse.masks import make_identity
+
+F32 = mybir.dt.float32
+BF16 = mybir.dt.bfloat16
+U32 = mybir.dt.uint32
+U8 = mybir.dt.uint8
+FP8 = mybir.dt.float8_e4m3fn
+FP8X4 = mybir.dt.float8_e4m3fn_x4
+ACT = mybir.ActivationFunctionType
+ALU = mybir.AluOpType
+
+B, K, O = 512, 2048, 2048
+C = 0.01 * 0.001 / 1
+FLOPS = 2 * B * K * O
+
+P = 128
+G = K // 512
+NJ = O // P
+NR = B // P
+
+LAG_WT = 1
+LAG_Q = 2
+LAG_MX = 3
+GROUPS = [[0], [1], [2, 3], [4, 5], [6, 7], [8, 9], [10, 11], [12, 13], [14], [15]]
+LAG_STT = 7
+LAG_OT = 8
+
+
+def tile_optimalnet_pb_kernel(tc, vi, W_bytes, W_scale, b, out_0, out_1):
+    nc = tc.nc
+    with ExitStack() as ctx:
+        const = ctx.enter_context(tc.tile_pool(name="const", bufs=1))
+        wbp = ctx.enter_context(tc.tile_pool(name="wbp", bufs=1))
+        wscp = ctx.enter_context(tc.tile_pool(name="wscp", bufs=6))
+        wgp = ctx.enter_context(tc.tile_pool(name="wgp", bufs=4))
+        wcp = ctx.enter_context(tc.tile_pool(name="wcp", bufs=5))
+        vjp = ctx.enter_context(tc.tile_pool(name="vjp", bufs=LAG_STT - LAG_MX + 3))
+        otp = ctx.enter_context(tc.tile_pool(name="otp", bufs=4))
+        osp = ctx.enter_context(tc.tile_pool(name="osp", bufs=8))
+        psx = ctx.enter_context(tc.psum_pool(name="psx", bufs=4))
+        psa = ctx.enter_context(tc.psum_pool(name="psa", bufs=2))
+        pso = ctx.enter_context(tc.psum_pool(name="pso", bufs=2))
+        ctx.enter_context(tc.manual_schedule(engines={mybir.EngineType.PE}))
+
+        ident_f = const.tile([P, P], F32, name="ident_f")
+        make_identity(nc, ident_f[:])
+        ident_b = const.tile([P, P], BF16, name="ident_b")
+        make_identity(nc, ident_b[:])
+        warm = const.tile([P, 1], F32, name="warm")
+        nc.vector.memset(warm[:], 0.0)
+        warm2 = const.tile([P, 1], F32, name="warm2")
+        nc.scalar.activation(out=warm2[:], in_=warm[:], func=ACT.Relu)
+        b_rows = const.tile([P, P], BF16, name="b_rows")
+        nc.gpsimd.memset(b_rows[:], 0.0)
+        m_cols = const.tile([P, P], F32, name="m_cols")
+        nc.gpsimd.memset(m_cols[:], 0.0)
+
+        scale_bc = const.tile([P, K], F32, name="scale_bc")
+        scale_row = W_scale.rearrange("o k -> (o k)")
+        wb = {}
+        vi_sb = {}
+
+        def load_scale(c):
+            nc.sync.dma_start(out=scale_bc[:, c * 512:(c + 1) * 512],
+                              in_=scale_row[c * 512:(c + 1) * 512].partition_broadcast(P))
+
+        def load_w(j):
+            wb[j] = wbp.tile([P, K], U8, name="wb%d" % j)
+            nc.sync.dma_start(out=wb[j][:], in_=W_bytes[j * P:(j + 1) * P, :])
+
+        def load_vi(rt):
+            vi_sb[rt] = const.tile([P, K], BF16, name="vi_sb%d" % rt)
+            nc.sync.dma_start(out=vi_sb[rt][:], in_=vi[rt * P:(rt + 1) * P, :])
+
+        load_scale(0)
+        load_w(0)
+        nc.sync.dma_start(out=b_rows[0:NJ, :], in_=b.rearrange("(j p) -> j p", p=P))
+        load_scale(1)
+        load_scale(2)
+        load_scale(3)
+        load_w(1)
+        load_vi(0)
+        load_w(2)
+        load_vi(1)
+        load_vi(2)
+        load_w(3)
+        load_vi(3)
+        for j in range(4, NJ):
+            load_w(j)
+
+        vi_grp = const.tile([P, G * B * 4], BF16, name="vi_grp", align_bytes=64)
+        vi_grp_w = vi_grp[:].bitcast(F32).rearrange("p (g r u) -> p g r u", g=G, u=2)
+        vi_cod = const.tile([P, G * B], U32, name="vi_cod", align_bytes=64)
+        vi_scl = const.tile([P, G * B], U8, name="vi_scl", align_bytes=64)
+
+        def transpose_words(words):
+            banks = []
+            for gp in range(2):
+                xt = psx.tile([P, 2, 2, P], F32, name="xt")
+                for gl in range(2):
+                    g = 2 * gp + gl
+                    for u in range(2):
+                        nc.tensor.transpose(xt[:, gl, u, :], words[:, 256 * g + u:256 * (g + 1):2], ident_f[:])
+                banks.append(xt)
+            return banks
+
+        def vi_turn(rt):
+            banks = transpose_words(vi_sb[rt][:].bitcast(F32))
+            for gp in range(2):
+                nc.scalar.copy(out=vi_grp_w[:, 2 * gp:2 * gp + 2, rt * P:(rt + 1) * P, :],
+                               in_=banks[gp][:].rearrange("p g u r -> p g r u"))
+
+        def vi_quant():
+            for g in range(G):
+                c0 = g * B
+                nc.vector.quantize_mx(out=vi_cod[:, c0:c0 + B].bitcast(FP8X4), scales=vi_scl[:, c0:c0 + B],
+                                      in_=vi_grp[:, 4 * c0:4 * (c0 + B)])
+
+        b_col = const.tile([P, NJ], F32, name="b_col")
+
+        def b_turn():
+            b_ps = pso.tile([P, P], BF16, name="b_ps", tag="ob")
+            nc.tensor.transpose(b_ps[:], b_rows[:], ident_b[:])
+            nc.scalar.copy(out=b_col[:], in_=b_ps[:, 0:NJ])
+
+        rs4 = const.tile([P, NR], F32, name="rs4")
+        junk = const.tile([P, K], BF16, name="junk")
+        rs_bc = const.tile([P, B], F32, name="rs_bc")
+
+        def row_sum(rt):
+            nc.scalar.activation(out=junk[:], in_=vi_sb[rt][:], func=ACT.Copy, accum_out=rs4[:, rt:rt + 1])
+
+        def row_sum_spread():
+            rs_ps = pso.tile([P, B], F32, name="rs_ps", tag="ob")
+            for rt in range(NR):
+                nc.tensor.matmul(rs_ps[:, rt * P:(rt + 1) * P], lhsT=rs4[:, rt:rt + 1].to_broadcast([P, P]),
+                                 rhs=ident_f[:], start=True, stop=True)
+            nc.scalar.mul(out=rs_bc[:], in_=rs_ps[:], mul=C / B)
+
+        sums = const.tile([P, NJ], F32, name="sums")
+        wsc = {}
+        xts = {}
+        wgrp = {}
+        wcod = {}
+        wscl = {}
+        acc = {}
+        vjt = {}
+        ot = {}
+        ob = {}
+        out_v = out_0.rearrange("(t p) o -> p t o", p=P)
+
+        def st_tt(j):
+            wsc[j] = wscp.tile([P, K], BF16, name="wsc")
+            nchunk = 4 if j == 0 else 1
+            w = K // nchunk
+            for c in range(nchunk):
+                nc.vector.tensor_tensor(out=wsc[j][:, c * w:(c + 1) * w], in0=wb[j][:, c * w:(c + 1) * w].bitcast(FP8),
+                                        in1=scale_bc[:, c * w:(c + 1) * w], op=ALU.mult)
+
+        def st_wt(j):
+            xts[j] = transpose_words(wsc[j][:].bitcast(F32))
+
+        def st_ev(j):
+            wgrp[j] = wgp.tile([P, K], BF16, name="wgrp", align_bytes=64)
+            words = wgrp[j][:].bitcast(F32)
+            for gp in range(2):
+                nc.scalar.copy(out=words[:, gp * 512:(gp + 1) * 512].rearrange("p (g o u) -> p g o u", g=2, u=2),
+                               in_=xts[j][gp][:].rearrange("p g u o -> p g o u"))
+
+        def st_q(j):
+            wcod[j] = wcp.tile([P, G * P], U32, name="wcod", align_bytes=64)
+            wscl[j] = wcp.tile([P, G * P], U8, name="wscl", align_bytes=64)
+            nc.vector.quantize_mx(out=wcod[j][:].bitcast(FP8X4), scales=wscl[j][:], in_=wgrp[j][:])
+
+        def st_mx(j):
+            acc[j] = psa.tile([P, B], F32, name="acc")
+            for g in range(G):
+                nc.tensor.matmul_mx(out=acc[j][:], lhsT=wcod[j][:, g * P:(g + 1) * P].bitcast(FP8X4),
+                                    lhsT_scale=wscl[j][:, g * P:(g + 1) * P],
+                                    rhs=vi_cod[:, g * B:(g + 1) * B].bitcast(FP8X4),
+                                    rhs_scale=vi_scl[:, g * B:(g + 1) * B], start=(g == 0), stop=(g == G - 1))
+
+        def st_relu(j):
+            vjt[j] = vjp.tile([P, B], F32, name="vjt")
+            nc.scalar.activation(out=vjt[j][:], in_=acc[j][:], func=ACT.Relu, bias=b_col[:, j:j + 1], scale=1.0,
+                                 accum_out=sums[:, j:j + 1])
+
+        def st_stt(j):
+            ot[j] = otp.tile([P, B], F32, name="ot")
+            nc.vector.scalar_tensor_tensor(out=ot[j][:], in0=rs_bc[:], scalar=sums[:, j:j + 1], in1=vjt[j][:],
+                                           op0=ALU.mult, op1=ALU.add)
+
+        def st_ot(j):
+            ob[j] = pso.tile([P, NR, P], F32, name="ob", tag="ob")
+            for rt in range(NR):
+                nc.tensor.transpose(ob[j][:, rt, :], ot[j][:, rt * P:(rt + 1) * P], ident_f[:])
+
+        def st_oev(j):
+            osb = osp.tile([P, NR, P], F32, name="osb")
+            nc.scalar.copy(out=osb[:], in_=ob[j][:])
+            nc.sync.dma_start(out=out_v[:, :, j * P:(j + 1) * P], in_=osb[:])
+
+        def m_scale():
+            nc.scalar.mul(out=m_cols[:, 0:NJ], in_=sums[:], mul=1.0 / B)
+
+        def m_store():
+            m_ps = pso.tile([P, P], F32, name="m_ps", tag="ob")
+            nc.tensor.transpose(m_ps[:], m_cols[:], ident_f[:])
+            m_rows = const.tile([P, P], F32, name="m_rows")
+            nc.scalar.copy(out=m_rows[0:NJ, :], in_=m_ps[0:NJ, :])
+            nc.sync.dma_start(out=out_1.rearrange("(j p) -> j p", p=P), in_=m_rows[0:NJ, :])
+
+        def run(fn, j):
+            if 0 <= j < NJ:
+                fn(j)
+
+        for s in range(NJ + LAG_OT):
+            run(st_tt, s)
+            run(st_q, s - LAG_Q)
+            run(st_stt, s - LAG_STT)
+            if 2 <= s <= 5:
+                row_sum(s - 2)
+            if s == NJ + LAG_MX + 1:
+                m_store()
+            run(st_ot, s - LAG_OT)
+            run(st_oev, s - LAG_OT)
+            if s == 2:
+                vi_turn(1)
+            if s == 3:
+                vi_turn(2)
+                vi_turn(3)
+                vi_quant()
+            run(st_wt, s - LAG_WT)
+            run(st_ev, s - LAG_WT)
+            if s == 1:
+                vi_turn(0)
+                b_turn()
+            for grp in GROUPS:
+                if grp[-1] == s - LAG_MX:
+                    for j in grp:
+                        st_mx(j)
+                        st_relu(j)
+            if s == NJ - 1 + LAG_MX:
+                m_scale()
+            if s == 6:
+                row_sum_spread()

@@ -63,9 +63,17 @@ def tile_optimalnet_pb_kernel(tc, vi, W_bytes, W_scale, b, out_0, out_1):
         wb = {}
         vi_sb = {}
 
-        def load_scale(c):
-            nc.sync.dma_start(out=scale_bc[:, c * 512:(c + 1) * 512],
-                              in_=scale_row[c * 512:(c + 1) * 512].partition_broadcast(P))
+        srow = const.tile([P, 512], F32, name="srow")
+        nc.vector.memset(srow[:], 0.0)
+        nc.sync.dma_start(out=srow[0:G, :], in_=scale_row.rearrange("(c n) -> c n", n=512))
+
+        def spread_scale(c):
+            sp = psx.tile([P, 512], F32, name="sp", tag="xt")
+            nc.tensor.matmul(sp[:], lhsT=ident_f[:, c:c + 1].to_broadcast([P, P]), rhs=srow[:], start=True, stop=True)
+            if c % 2 == 0:
+                nc.vector.tensor_copy(out=scale_bc[:, c * 512:(c + 1) * 512], in_=sp[:])
+            else:
+                nc.scalar.copy(out=scale_bc[:, c * 512:(c + 1) * 512], in_=sp[:])
 
         def load_w(j):
             wb[j] = wbp.tile([P, K], U8, name="wb%d" % j)
@@ -75,12 +83,10 @@ def tile_optimalnet_pb_kernel(tc, vi, W_bytes, W_scale, b, out_0, out_1):
             vi_sb[rt] = const.tile([P, K], BF16, name="vi_sb%d" % rt)
             nc.sync.dma_start(out=vi_sb[rt][:], in_=vi[rt * P:(rt + 1) * P, :])
 
-        load_scale(0)
         load_w(0)
         nc.sync.dma_start(out=b_rows[0:NJ, :], in_=b.rearrange("(j p) -> j p", p=P))
-        load_scale(1)
-        load_scale(2)
-        load_scale(3)
+        for c in range(G):
+            spread_scale(c)
         load_w(1)
         load_vi(0)
         load_w(2)
@@ -99,7 +105,7 @@ def tile_optimalnet_pb_kernel(tc, vi, W_bytes, W_scale, b, out_0, out_1):
         def transpose_words(words):
             banks = []
             for gp in range(2):
-                xt = psx.tile([P, 2, 2, P], F32, name="xt")
+                xt = psx.tile([P, 2, 2, P], F32, name="xt", tag="xt")
                 for gl in range(2):
                     g = 2 * gp + gl
                     for u in range(2):

@@ -63,17 +63,21 @@ def tile_optimalnet_pb_kernel(tc, vi, W_bytes, W_scale, b, out_0, out_1):
         wb = {}
         vi_sb = {}
 
-        srow = const.tile([P, 512], F32, name="srow")
-        nc.vector.memset(srow[:], 0.0)
-        nc.sync.dma_start(out=srow[0:G, :], in_=scale_row.rearrange("(c n) -> c n", n=512))
+        s_rows = const.tile([P, P], F32, name="s_rows")
+        nc.vector.memset(s_rows[:], 0.0)
+        nc.sync.dma_start(out=s_rows[0:K // P, :], in_=scale_row.rearrange("(c p) -> c p", p=P))
+        s_col = const.tile([P, K // P], F32, name="s_col")
+
+        def scale_turn():
+            s_ps = psx.tile([P, P], F32, name="s_ps", tag="xt")
+            nc.tensor.transpose(s_ps[:], s_rows[:], ident_f[:])
+            nc.scalar.copy(out=s_col[:], in_=s_ps[:, 0:K // P])
 
         def spread_scale(c):
-            sp = psx.tile([P, 512], F32, name="sp", tag="xt")
-            nc.tensor.matmul(sp[:], lhsT=ident_f[:, c:c + 1].to_broadcast([P, P]), rhs=srow[:], start=True, stop=True)
-            if c % 2 == 0:
-                nc.vector.tensor_copy(out=scale_bc[:, c * 512:(c + 1) * 512], in_=sp[:])
-            else:
-                nc.scalar.copy(out=scale_bc[:, c * 512:(c + 1) * 512], in_=sp[:])
+            sp = psx.tile([P, 4, P], F32, name="sp", tag="xt")
+            for q in range(4):
+                nc.tensor.transpose(sp[:, q, :], s_col[:, 4 * c + q:4 * c + q + 1].to_broadcast([P, P]), ident_f[:])
+            nc.scalar.copy(out=scale_bc[:, c * 512:(c + 1) * 512], in_=sp[:].rearrange("p q n -> p (q n)"))
 
         def load_w(j):
             wb[j] = wbp.tile([P, K], U8, name="wb%d" % j)
@@ -85,6 +89,7 @@ def tile_optimalnet_pb_kernel(tc, vi, W_bytes, W_scale, b, out_0, out_1):
 
         load_w(0)
         nc.sync.dma_start(out=b_rows[0:NJ, :], in_=b.rearrange("(j p) -> j p", p=P))
+        scale_turn()
         for c in range(G):
             spread_scale(c)
         load_w(1)

@@ -26,7 +26,8 @@ LAG_Q = 2
 LAG_MX = 3
 GROUPS = [[0], [1], [2, 3], [4, 5], [6, 7], [8, 9], [10, 11], [12, 13], [14], [15]]
 LAG_STT = 7
-LAG_OT = 8
+RS_STEP = 4
+STT_FIRST = RS_STEP + NR
 
 
 def tile_optimalnet_pb_kernel(tc, vi, W_bytes, W_scale, b, out_0, out_1):
@@ -37,13 +38,13 @@ def tile_optimalnet_pb_kernel(tc, vi, W_bytes, W_scale, b, out_0, out_1):
         wscp = ctx.enter_context(tc.tile_pool(name="wscp", bufs=6))
         wgp = ctx.enter_context(tc.tile_pool(name="wgp", bufs=4))
         wcp = ctx.enter_context(tc.tile_pool(name="wcp", bufs=5))
-        vjp = ctx.enter_context(tc.tile_pool(name="vjp", bufs=LAG_STT - LAG_MX + 3))
+        vjp = ctx.enter_context(tc.tile_pool(name="vjp", bufs=LAG_STT - LAG_MX + 5))
         otp = ctx.enter_context(tc.tile_pool(name="otp", bufs=4))
         osp = ctx.enter_context(tc.tile_pool(name="osp", bufs=8))
         psx = ctx.enter_context(tc.psum_pool(name="psx", bufs=4))
         psa = ctx.enter_context(tc.psum_pool(name="psa", bufs=2))
         pso = ctx.enter_context(tc.psum_pool(name="pso", bufs=2))
-        ctx.enter_context(tc.manual_schedule(engines={mybir.EngineType.PE}))
+        ctx.enter_context(tc.manual_schedule(engines={mybir.EngineType.PE, mybir.EngineType.Activation}))
 
         ident_f = const.tile([P, P], F32, name="ident_f")
         make_identity(nc, ident_f[:])
@@ -228,16 +229,21 @@ def tile_optimalnet_pb_kernel(tc, vi, W_bytes, W_scale, b, out_0, out_1):
             if 0 <= j < NJ:
                 fn(j)
 
-        for s in range(NJ + LAG_OT):
+        def stt_step(j):
+            return max(j + LAG_STT, STT_FIRST)
+
+        for s in range(NJ + LAG_STT + 1):
             run(st_tt, s)
             run(st_q, s - LAG_Q)
-            run(st_stt, s - LAG_STT)
-            if 2 <= s <= 5:
-                row_sum(s - 2)
+            for j in range(NJ):
+                if stt_step(j) == s:
+                    st_stt(j)
             if s == NJ + LAG_MX + 1:
                 m_store()
-            run(st_ot, s - LAG_OT)
-            run(st_oev, s - LAG_OT)
+            for j in range(NJ):
+                if stt_step(j) + 1 == s:
+                    st_ot(j)
+                    st_oev(j)
             if s == 2:
                 vi_turn(1)
             if s == 3:
@@ -256,5 +262,7 @@ def tile_optimalnet_pb_kernel(tc, vi, W_bytes, W_scale, b, out_0, out_1):
                         st_relu(j)
             if s == NJ - 1 + LAG_MX:
                 m_scale()
-            if s == 6:
+            if RS_STEP <= s < RS_STEP + NR:
+                row_sum(s - RS_STEP)
+            if s == RS_STEP + NR - 1:
                 row_sum_spread()

@@ -148,8 +148,7 @@ def tile_optimalnet_pb_kernel(tc, vi, W_bytes, W_scale, b, out_0, out_1):
         def row_sum_spread():
             rs_ps = pso.tile([P, B], F32, name="rs_ps", tag="ob")
             for rt in range(NR):
-                nc.tensor.matmul(rs_ps[:, rt * P:(rt + 1) * P], lhsT=rs4[:, rt:rt + 1].to_broadcast([P, P]),
-                                 rhs=ident_f[:], start=True, stop=True)
+                nc.tensor.transpose(rs_ps[:, rt * P:(rt + 1) * P], rs4[:, rt:rt + 1].to_broadcast([P, P]), ident_f[:])
             nc.scalar.mul(out=rs_bc[:], in_=rs_ps[:], mul=C / B)
 
         sums = const.tile([P, NJ], F32, name="sums")

@@ -19,15 +19,11 @@ FLOPS = 2 * B * K * O
 P = 128
 G = K // 512
 NJ = O // P
+NQ = NJ // 2
+PW = 2 * P
 NR = B // P
 
-LAG_WT = 1
-LAG_Q = 2
-LAG_MX = 3
-GROUPS = [[0], [1], [2, 3], [4, 5], [6, 7], [8, 9], [10, 11], [12, 13], [14], [15]]
-LAG_STT = 7
-RS_STEP = 4
-STT_FIRST = RS_STEP + NR
+POOL_CASTS = (2, 3, 4, 5, 6, 7, 10, 12, 14)
 
 
 def tile_optimalnet_pb_kernel(tc, vi, W_bytes, W_scale, b, out_0, out_1):
@@ -35,15 +31,15 @@ def tile_optimalnet_pb_kernel(tc, vi, W_bytes, W_scale, b, out_0, out_1):
     with ExitStack() as ctx:
         const = ctx.enter_context(tc.tile_pool(name="const", bufs=1))
         wbp = ctx.enter_context(tc.tile_pool(name="wbp", bufs=1))
-        wscp = ctx.enter_context(tc.tile_pool(name="wscp", bufs=6))
-        wgp = ctx.enter_context(tc.tile_pool(name="wgp", bufs=4))
-        wcp = ctx.enter_context(tc.tile_pool(name="wcp", bufs=5))
-        vjp = ctx.enter_context(tc.tile_pool(name="vjp", bufs=LAG_STT - LAG_MX + 5))
-        otp = ctx.enter_context(tc.tile_pool(name="otp", bufs=4))
-        osp = ctx.enter_context(tc.tile_pool(name="osp", bufs=8))
-        psx = ctx.enter_context(tc.psum_pool(name="psx", bufs=4))
+        wkp = ctx.enter_context(tc.tile_pool(name="wkp", bufs=NJ))
+        wgp = ctx.enter_context(tc.tile_pool(name="wgp", bufs=3))
+        wcp = ctx.enter_context(tc.tile_pool(name="wcp", bufs=3))
+        vjp = ctx.enter_context(tc.tile_pool(name="vjp", bufs=6))
+        osp = ctx.enter_context(tc.tile_pool(name="osp", bufs=4))
+        psx = ctx.enter_context(tc.psum_pool(name="psx", bufs=3))
         psa = ctx.enter_context(tc.psum_pool(name="psa", bufs=2))
         pso = ctx.enter_context(tc.psum_pool(name="pso", bufs=2))
+        psm = ctx.enter_context(tc.psum_pool(name="psm", bufs=1))
         ctx.enter_context(tc.manual_schedule(engines={mybir.EngineType.PE, mybir.EngineType.Activation}))
 
         ident_f = const.tile([P, P], F32, name="ident_f")
@@ -56,29 +52,10 @@ def tile_optimalnet_pb_kernel(tc, vi, W_bytes, W_scale, b, out_0, out_1):
         nc.scalar.activation(out=warm2[:], in_=warm[:], func=ACT.Relu)
         b_rows = const.tile([P, P], BF16, name="b_rows")
         nc.gpsimd.memset(b_rows[:], 0.0)
-        m_cols = const.tile([P, P], F32, name="m_cols")
-        nc.gpsimd.memset(m_cols[:], 0.0)
 
-        scale_bc = const.tile([P, K], F32, name="scale_bc")
-        scale_row = W_scale.rearrange("o k -> (o k)")
         wb = {}
         vi_sb = {}
-
-        s_rows = const.tile([P, P], F32, name="s_rows")
-        nc.vector.memset(s_rows[:], 0.0)
-        nc.sync.dma_start(out=s_rows[0:K // P, :], in_=scale_row.rearrange("(c p) -> c p", p=P))
-        s_col = const.tile([P, K // P], F32, name="s_col")
-
-        def scale_turn():
-            s_ps = psx.tile([P, P], F32, name="s_ps", tag="xt")
-            nc.tensor.transpose(s_ps[:], s_rows[:], ident_f[:])
-            nc.scalar.copy(out=s_col[:], in_=s_ps[:, 0:K // P])
-
-        def spread_scale(c):
-            sp = psx.tile([P, 4, P], F32, name="sp", tag="xt")
-            for q in range(4):
-                nc.tensor.transpose(sp[:, q, :], s_col[:, 4 * c + q:4 * c + q + 1].to_broadcast([P, P]), ident_f[:])
-            nc.scalar.copy(out=scale_bc[:, c * 512:(c + 1) * 512], in_=sp[:].rearrange("p q n -> p (q n)"))
+        s_t = const.tile([P, G, 4], F32, name="s_t")
 
         def load_w(j):
             wb[j] = wbp.tile([P, K], U8, name="wb%d" % j)
@@ -89,16 +66,14 @@ def tile_optimalnet_pb_kernel(tc, vi, W_bytes, W_scale, b, out_0, out_1):
             nc.sync.dma_start(out=vi_sb[rt][:], in_=vi[rt * P:(rt + 1) * P, :])
 
         load_w(0)
-        nc.sync.dma_start(out=b_rows[0:NJ, :], in_=b.rearrange("(j p) -> j p", p=P))
-        scale_turn()
-        for c in range(G):
-            spread_scale(c)
+        nc.scalar.dma_start(out=s_t[:], in_=W_scale.rearrange("o (g p t) -> p (o g) t", p=P, t=4))
+        nc.scalar.dma_start(out=b_rows[0:NJ, :], in_=b.rearrange("(j p) -> j p", p=P))
         load_w(1)
-        load_vi(0)
         load_w(2)
+        load_vi(0)
+        load_w(3)
         load_vi(1)
         load_vi(2)
-        load_w(3)
         load_vi(3)
         for j in range(4, NJ):
             load_w(j)
@@ -108,22 +83,17 @@ def tile_optimalnet_pb_kernel(tc, vi, W_bytes, W_scale, b, out_0, out_1):
         vi_cod = const.tile([P, G * B], U32, name="vi_cod", align_bytes=64)
         vi_scl = const.tile([P, G * B], U8, name="vi_scl", align_bytes=64)
 
-        def transpose_words(words):
-            banks = []
+        def vi_turn(rt):
+            words = vi_sb[rt][:].bitcast(F32)
+            pool, tag = ((psa, "acc"), (pso, "ob"))[rt % 2]
             for gp in range(2):
-                xt = psx.tile([P, 2, 2, P], F32, name="xt", tag="xt")
+                xv = pool.tile([P, 2, 2, P], F32, name="xv", tag=tag)
                 for gl in range(2):
                     g = 2 * gp + gl
                     for u in range(2):
-                        nc.tensor.transpose(xt[:, gl, u, :], words[:, 256 * g + u:256 * (g + 1):2], ident_f[:])
-                banks.append(xt)
-            return banks
-
-        def vi_turn(rt):
-            banks = transpose_words(vi_sb[rt][:].bitcast(F32))
-            for gp in range(2):
+                        nc.tensor.transpose(xv[:, gl, u, :], words[:, 256 * g + u:256 * (g + 1):2], ident_f[:])
                 nc.scalar.copy(out=vi_grp_w[:, 2 * gp:2 * gp + 2, rt * P:(rt + 1) * P, :],
-                               in_=banks[gp][:].rearrange("p g u r -> p g r u"))
+                               in_=xv[:].rearrange("p g u r -> p g r u"))
 
         def vi_quant():
             for g in range(G):
@@ -134,134 +104,176 @@ def tile_optimalnet_pb_kernel(tc, vi, W_bytes, W_scale, b, out_0, out_1):
         b_col = const.tile([P, NJ], F32, name="b_col")
 
         def b_turn():
-            b_ps = pso.tile([P, P], BF16, name="b_ps", tag="ob")
+            b_ps = psm.tile([P, P], BF16, name="b_ps", tag="sm")
             nc.tensor.transpose(b_ps[:], b_rows[:], ident_b[:])
             nc.scalar.copy(out=b_col[:], in_=b_ps[:, 0:NJ])
 
-        rs4 = const.tile([P, NR], F32, name="rs4")
+        rsc = const.tile([P, NR], F32, name="rsc")
         junk = const.tile([P, K], BF16, name="junk")
-        rs_bc = const.tile([P, B], F32, name="rs_bc")
 
         def row_sum(rt):
-            nc.scalar.activation(out=junk[:], in_=vi_sb[rt][:], func=ACT.Copy, accum_out=rs4[:, rt:rt + 1])
-
-        def row_sum_spread():
-            rs_ps = pso.tile([P, B], F32, name="rs_ps", tag="ob")
-            for rt in range(NR):
-                nc.tensor.transpose(rs_ps[:, rt * P:(rt + 1) * P], rs4[:, rt:rt + 1].to_broadcast([P, P]), ident_f[:])
-            nc.scalar.mul(out=rs_bc[:], in_=rs_ps[:], mul=C / B)
+            nc.scalar.activation(out=junk[:], in_=vi_sb[rt][:], func=ACT.Copy, scale=C, accum_out=rsc[:, rt:rt + 1])
 
         sums = const.tile([P, NJ], F32, name="sums")
-        wsc = {}
-        xts = {}
+        m_all = const.tile([P, O], F32, name="m_all")
+        wk = {}
+        xt = {}
         wgrp = {}
         wcod = {}
         wscl = {}
         acc = {}
         vjt = {}
-        ot = {}
         ob = {}
         out_v = out_0.rearrange("(t p) o -> p t o", p=P)
 
-        def st_tt(j):
-            wsc[j] = wscp.tile([P, K], BF16, name="wsc")
-            nchunk = 4 if j == 0 else 1
-            w = K // nchunk
-            for c in range(nchunk):
-                nc.vector.tensor_tensor(out=wsc[j][:, c * w:(c + 1) * w], in0=wb[j][:, c * w:(c + 1) * w].bitcast(FP8),
-                                        in1=scale_bc[:, c * w:(c + 1) * w], op=ALU.mult)
+        def cast(fn, j, k0, k1):
+            fn(out=wk[j][:, k0:k1], in_=wb[j][:, k0:k1].bitcast(FP8))
 
-        def st_wt(j):
-            xts[j] = transpose_words(wsc[j][:].bitcast(F32))
+        def st_cast(j):
+            wk[j] = wkp.tile([P, K], BF16, name="wk")
+            cast(nc.gpsimd.tensor_copy if j in POOL_CASTS else nc.scalar.copy, j, 0, K)
 
-        def st_ev(j):
-            wgrp[j] = wgp.tile([P, K], BF16, name="wgrp", align_bytes=64)
-            words = wgrp[j][:].bitcast(F32)
-            for gp in range(2):
-                nc.scalar.copy(out=words[:, gp * 512:(gp + 1) * 512].rearrange("p (g o u) -> p g o u", g=2, u=2),
-                               in_=xts[j][gp][:].rearrange("p g u o -> p g o u"))
+        def first_casts():
+            for j in range(2):
+                wk[j] = wkp.tile([P, K], BF16, name="wk")
+            cast(nc.vector.tensor_copy, 0, 0, 512)
+            cast(nc.vector.tensor_copy, 1, 0, 512)
+            cast(nc.scalar.copy, 1, 512, K)
+            cast(nc.vector.tensor_copy, 0, 512, K)
 
-        def st_q(j):
-            wcod[j] = wcp.tile([P, G * P], U32, name="wcod", align_bytes=64)
-            wscl[j] = wcp.tile([P, G * P], U8, name="wscl", align_bytes=64)
-            nc.vector.quantize_mx(out=wcod[j][:].bitcast(FP8X4), scales=wscl[j][:], in_=wgrp[j][:])
+        def st_wt(q, g):
+            xt[q, g] = psx.tile([P, 2, PW], F32, name="xt")
+            for a in range(2):
+                words = wk[2 * q + a][:].bitcast(F32)
+                for u in range(2):
+                    nc.tensor.transpose(xt[q, g][:, u, a * P:(a + 1) * P], words[:, 256 * g + u:256 * (g + 1):2],
+                                        ident_f[:])
 
-        def st_mx(j):
-            acc[j] = psa.tile([P, B], F32, name="acc")
-            for g in range(G):
-                nc.tensor.matmul_mx(out=acc[j][:], lhsT=wcod[j][:, g * P:(g + 1) * P].bitcast(FP8X4),
-                                    lhsT_scale=wscl[j][:, g * P:(g + 1) * P],
+        def st_prod(q, g):
+            if g == 0:
+                wgrp[q] = wgp.tile([P, G * PW * 4], BF16, name="wgrp", align_bytes=64)
+            w = PW * 4
+            nc.vector.tensor_tensor(
+                out=wgrp[q][:, g * w:(g + 1) * w].rearrange("p (o u e) -> p o u e", u=2, e=2),
+                in0=xt[q, g][:].bitcast(BF16).rearrange("p u (o e) -> p o u e", e=2),
+                in1=s_t[:, g:g + 1, :].rearrange("p o (u e) -> p o u e", u=2).to_broadcast([P, PW, 2, 2]),
+                op=ALU.mult)
+
+        def st_q(q, g0, g1):
+            if g0 == 0:
+                wcod[q] = wcp.tile([P, G * PW], U32, name="wcod", align_bytes=64)
+                wscl[q] = wcp.tile([P, G * PW], U8, name="wscl", align_bytes=64)
+            c0, c1 = g0 * PW, g1 * PW
+            nc.vector.quantize_mx(out=wcod[q][:, c0:c1].bitcast(FP8X4), scales=wscl[q][:, c0:c1],
+                                  in_=wgrp[q][:, 4 * c0:4 * c1])
+
+        def mx_passes(q, a, g0, g1):
+            j = 2 * q + a
+            if g0 == 0:
+                acc[j] = psa.tile([P, B], F32, name="acc", tag="acc")
+            for g in range(g0, g1):
+                c0 = g * PW + a * P
+                nc.tensor.matmul_mx(out=acc[j][:], lhsT=wcod[q][:, c0:c0 + P].bitcast(FP8X4),
+                                    lhsT_scale=wscl[q][:, c0:c0 + P],
                                     rhs=vi_cod[:, g * B:(g + 1) * B].bitcast(FP8X4),
                                     rhs_scale=vi_scl[:, g * B:(g + 1) * B], start=(g == 0), stop=(g == G - 1))
+            if g1 == G:
+                vjt[j] = vjp.tile([P, B], F32, name="vjt")
+                nc.scalar.activation(out=vjt[j][:], in_=acc[j][:], func=ACT.Relu, bias=b_col[:, j:j + 1], scale=1.0,
+                                     accum_out=sums[:, j:j + 1])
 
-        def st_relu(j):
-            vjt[j] = vjp.tile([P, B], F32, name="vjt")
-            nc.scalar.activation(out=vjt[j][:], in_=acc[j][:], func=ACT.Relu, bias=b_col[:, j:j + 1], scale=1.0,
-                                 accum_out=sums[:, j:j + 1])
+        def st_mx(q):
+            for a in range(2):
+                mx_passes(q, a, 0, G)
 
-        def st_stt(j):
-            ot[j] = otp.tile([P, B], F32, name="ot")
-            nc.vector.scalar_tensor_tensor(out=ot[j][:], in0=rs_bc[:], scalar=sums[:, j:j + 1], in1=vjt[j][:],
-                                           op0=ALU.mult, op1=ALU.add)
+        def st_back(q):
+            m_ps = psm.tile([P, PW], F32, name="m_ps", tag="sm")
+            for a in range(2):
+                j = 2 * q + a
+                nc.tensor.transpose(m_ps[:, a * P:(a + 1) * P], sums[:, j:j + 1].to_broadcast([P, P]), ident_f[:])
+            for rp in range(2):
+                ob[q, rp] = pso.tile([P, 2, PW], F32, name="ob", tag="ob")
+                for rl in range(2):
+                    rt = 2 * rp + rl
+                    for a in range(2):
+                        nc.tensor.transpose(ob[q, rp][:, rl, a * P:(a + 1) * P],
+                                            vjt[2 * q + a][:, rt * P:(rt + 1) * P], ident_f[:])
+            nc.scalar.mul(out=m_all[:, q * PW:(q + 1) * PW], in_=m_ps[:], mul=1.0 / B)
 
-        def st_ot(j):
+        def st_out(q):
+            osb = osp.tile([P, NR, PW], F32, name="osb")
+            for rt in range(NR):
+                nc.vector.scalar_tensor_tensor(out=osb[:, rt, :], in0=m_all[:, q * PW:(q + 1) * PW],
+                                               scalar=rsc[:, rt:rt + 1], in1=ob[q, rt // 2][:, rt % 2, :],
+                                               op0=ALU.mult, op1=ALU.add)
+            nc.sync.dma_start(out=out_v[:, :, q * PW:(q + 1) * PW], in_=osb[:])
+
+        def last_back(a):
+            j = 2 * (NQ - 1) + a
+            m_ps = psm.tile([P, PW], F32, name="m_ps", tag="sm")
+            nc.tensor.transpose(m_ps[:, 0:P], sums[:, j:j + 1].to_broadcast([P, P]), ident_f[:])
+            nc.scalar.mul(out=m_all[:, j * P:(j + 1) * P], in_=m_ps[:, 0:P], mul=1.0 / B)
             ob[j] = pso.tile([P, NR, P], F32, name="ob", tag="ob")
             for rt in range(NR):
-                nc.tensor.transpose(ob[j][:, rt, :], ot[j][:, rt * P:(rt + 1) * P], ident_f[:])
+                nc.tensor.transpose(ob[j][:, rt, :], vjt[j][:, rt * P:(rt + 1) * P], ident_f[:])
 
-        def st_oev(j):
-            osb = osp.tile([P, NR, P], F32, name="osb")
-            nc.scalar.copy(out=osb[:], in_=ob[j][:])
+        def last_out(a):
+            j = 2 * (NQ - 1) + a
+            osb = osp.tile([P, NR, P], F32, name="osb_l")
+            for rt in range(NR):
+                nc.vector.scalar_tensor_tensor(out=osb[:, rt, :], in0=m_all[:, j * P:(j + 1) * P],
+                                               scalar=rsc[:, rt:rt + 1], in1=ob[j][:, rt, :],
+                                               op0=ALU.mult, op1=ALU.add)
             nc.sync.dma_start(out=out_v[:, :, j * P:(j + 1) * P], in_=osb[:])
 
-        def m_scale():
-            nc.scalar.mul(out=m_cols[:, 0:NJ], in_=sums[:], mul=1.0 / B)
+        NU = NQ * G
 
-        def m_store():
-            m_ps = pso.tile([P, P], F32, name="m_ps", tag="ob")
-            nc.tensor.transpose(m_ps[:], m_cols[:], ident_f[:])
-            m_rows = const.tile([P, P], F32, name="m_rows")
-            nc.scalar.copy(out=m_rows[0:NJ, :], in_=m_ps[0:NJ, :])
-            nc.sync.dma_start(out=out_1.rearrange("(j p) -> j p", p=P), in_=m_rows[0:NJ, :])
+        def run(fn, i):
+            if 0 <= i < NU:
+                fn(i // G, i % G)
 
-        def run(fn, j):
-            if 0 <= j < NJ:
-                fn(j)
+        def pair_at(i):
+            return i // G if i >= 0 and i % G == 0 and i // G < NQ - 1 else None
 
-        def stt_step(j):
-            return max(j + LAG_STT, STT_FIRST)
-
-        for s in range(NJ + LAG_STT + 1):
-            run(st_tt, s)
-            run(st_q, s - LAG_Q)
-            for j in range(NJ):
-                if stt_step(j) == s:
-                    st_stt(j)
-            if s == NJ + LAG_MX + 1:
-                m_store()
-            for j in range(NJ):
-                if stt_step(j) + 1 == s:
-                    st_ot(j)
-                    st_oev(j)
-            if s == 2:
-                vi_turn(1)
-            if s == 3:
-                vi_turn(2)
-                vi_turn(3)
+        first_casts()
+        for j in range(2, 6):
+            st_cast(j)
+        st_wt(0, 0)
+        st_wt(0, 1)
+        for i in range(NU + 1):
+            run(st_prod, i)
+            if i % 2 == 0 and 0 <= i - 2 < NU - 2:
+                st_q((i - 2) // G, (i - 2) % G, (i - 2) % G + 2)
+            if i == 6:
                 vi_quant()
-            run(st_wt, s - LAG_WT)
-            run(st_ev, s - LAG_WT)
-            if s == 1:
-                vi_turn(0)
+            if pair_at(i - 10) is not None:
+                st_out(pair_at(i - 10))
+            if i < NR:
+                vi_turn(i)
+            run(st_wt, i + 2)
+            if i == 0:
                 b_turn()
-            for grp in GROUPS:
-                if grp[-1] == s - LAG_MX:
-                    for j in grp:
-                        st_mx(j)
-                        st_relu(j)
-            if s == NJ - 1 + LAG_MX:
-                m_scale()
-            if RS_STEP <= s < RS_STEP + NR:
-                row_sum(s - RS_STEP)
-            if s == RS_STEP + NR - 1:
-                row_sum_spread()
+            for j in range(6, NJ):
+                if i == 4 * (j // 2) - 6 + j % 2:
+                    st_cast(j)
+            if pair_at(i - 8) is not None:
+                st_back(pair_at(i - 8))
+            if 4 <= i < 4 + NR:
+                row_sum(i - 4)
+            if i == 7:
+                st_mx(0)
+            elif i >= 9 and pair_at(i - 5) is not None:
+                st_mx(pair_at(i - 5))
+            if i == NU - 1:
+                for a in range(2):
+                    mx_passes(NQ - 1, a, 0, 2)
+
+        st_q(NQ - 1, 2, 3)
+        st_q(NQ - 1, 3, 4)
+        for a in range(2):
+            mx_passes(NQ - 1, a, 2, G)
+        st_out(NQ - 2)
+        for a in range(2):
+            last_back(a)
+            last_out(a)
+        nc.sync.dma_start(out=out_1.rearrange("(a o) -> a o", a=1), in_=m_all[0:1, :])

@@ -23,7 +23,25 @@ NQ = NJ // 2
 PW = 2 * P
 NR = B // P
 
-POOL_CASTS = (2, 3, 4, 5, 6, 7, 10, 12, 14)
+VQ, OUT, BACK, MX, MX0, OUT0 = 6, 11, 7, 4, 6, 15
+
+
+def mx_step(q):
+    return max(G * q + MX, MX0)
+
+
+def back_step(q):
+    return max(G * q + BACK, mx_step(q) + 1, OUT0 + 2 * q - 2)
+
+
+def out_step(q):
+    return max(G * q + OUT, back_step(q) + 1, OUT0 + 2 * q)
+
+
+RS = (4, 5, 6, 7)
+POOL_CASTS = (2, 3, 4, 5, 6, 7, 8, 9, 10)
+POOL_PAIRS = (2, 3, 4, 5, 6, 7)
+CL = 9
 
 
 def tile_optimalnet_pb_kernel(tc, vi, W_bytes, W_scale, b, out_0, out_1):
@@ -32,15 +50,18 @@ def tile_optimalnet_pb_kernel(tc, vi, W_bytes, W_scale, b, out_0, out_1):
         const = ctx.enter_context(tc.tile_pool(name="const", bufs=1))
         wbp = ctx.enter_context(tc.tile_pool(name="wbp", bufs=1))
         wkp = ctx.enter_context(tc.tile_pool(name="wkp", bufs=NJ))
+        wip = ctx.enter_context(tc.tile_pool(name="wip", bufs=2))
         wgp = ctx.enter_context(tc.tile_pool(name="wgp", bufs=3))
         wcp = ctx.enter_context(tc.tile_pool(name="wcp", bufs=3))
         vjp = ctx.enter_context(tc.tile_pool(name="vjp", bufs=6))
         osp = ctx.enter_context(tc.tile_pool(name="osp", bufs=4))
-        psx = ctx.enter_context(tc.psum_pool(name="psx", bufs=3))
+        psx = ctx.enter_context(tc.psum_pool(name="psx", bufs=4))
         psa = ctx.enter_context(tc.psum_pool(name="psa", bufs=2))
         pso = ctx.enter_context(tc.psum_pool(name="pso", bufs=2))
-        psm = ctx.enter_context(tc.psum_pool(name="psm", bufs=1))
-        ctx.enter_context(tc.manual_schedule(engines={mybir.EngineType.PE, mybir.EngineType.Activation}))
+        ctx.enter_context(tc.manual_schedule(engines={mybir.EngineType.PE, mybir.EngineType.Activation, mybir.EngineType.DVE}))
+
+        s_t = const.tile([P, G, 4], F32, name="s_t")
+        nc.scalar.dma_start(out=s_t[:], in_=W_scale.rearrange("o (g p t) -> p (o g) t", p=P, t=4))
 
         ident_f = const.tile([P, P], F32, name="ident_f")
         make_identity(nc, ident_f[:])
@@ -55,7 +76,6 @@ def tile_optimalnet_pb_kernel(tc, vi, W_bytes, W_scale, b, out_0, out_1):
 
         wb = {}
         vi_sb = {}
-        s_t = const.tile([P, G, 4], F32, name="s_t")
 
         def load_w(j):
             wb[j] = wbp.tile([P, K], U8, name="wb%d" % j)
@@ -66,11 +86,10 @@ def tile_optimalnet_pb_kernel(tc, vi, W_bytes, W_scale, b, out_0, out_1):
             nc.sync.dma_start(out=vi_sb[rt][:], in_=vi[rt * P:(rt + 1) * P, :])
 
         load_w(0)
-        nc.scalar.dma_start(out=s_t[:], in_=W_scale.rearrange("o (g p t) -> p (o g) t", p=P, t=4))
-        nc.scalar.dma_start(out=b_rows[0:NJ, :], in_=b.rearrange("(j p) -> j p", p=P))
         load_w(1)
         load_w(2)
         load_vi(0)
+        nc.sync.dma_start(out=b_rows[0:NJ, :], in_=b.rearrange("(j p) -> j p", p=P))
         load_w(3)
         load_vi(1)
         load_vi(2)
@@ -104,7 +123,7 @@ def tile_optimalnet_pb_kernel(tc, vi, W_bytes, W_scale, b, out_0, out_1):
         b_col = const.tile([P, NJ], F32, name="b_col")
 
         def b_turn():
-            b_ps = psm.tile([P, P], BF16, name="b_ps", tag="sm")
+            b_ps = psx.tile([P, P], BF16, name="b_ps", tag="xt")
             nc.tensor.transpose(b_ps[:], b_rows[:], ident_b[:])
             nc.scalar.copy(out=b_col[:], in_=b_ps[:, 0:NJ])
 
@@ -142,16 +161,30 @@ def tile_optimalnet_pb_kernel(tc, vi, W_bytes, W_scale, b, out_0, out_1):
             cast(nc.vector.tensor_copy, 0, 512, K)
 
         def st_wt(q, g):
-            xt[q, g] = psx.tile([P, 2, PW], F32, name="xt")
+            xt[q, g] = psx.tile([P, 2, PW], F32, name="xt", tag="xt")
             for a in range(2):
                 words = wk[2 * q + a][:].bitcast(F32)
                 for u in range(2):
                     nc.tensor.transpose(xt[q, g][:, u, a * P:(a + 1) * P], words[:, 256 * g + u:256 * (g + 1):2],
                                         ident_f[:])
 
+        def st_wgrp(q):
+            wgrp[q] = wgp.tile([P, G * PW * 4], BF16, name="wgrp", align_bytes=64)
+
+        def st_pool(q, g):
+            w = PW * 4
+            wint = wip.tile([P, w], BF16, name="wint", align_bytes=64)
+            nc.scalar.copy(out=wint[:].bitcast(F32).rearrange("p (o u) -> p o u", u=2),
+                           in_=xt[q, g][:].rearrange("p u o -> p o u"))
+            nc.gpsimd.tensor_tensor(out=wgrp[q][:, g * w:(g + 1) * w].rearrange("p (o t) -> p o t", t=4),
+                                    in0=wint[:].rearrange("p (o t) -> p o t", t=4),
+                                    in1=s_t[:, g:g + 1, :].to_broadcast([P, PW, 4]), op=ALU.mult)
+
         def st_prod(q, g):
-            if g == 0:
-                wgrp[q] = wgp.tile([P, G * PW * 4], BF16, name="wgrp", align_bytes=64)
+            if q in POOL_PAIRS and g == G - 1:
+                return
+            if g == 0 and q not in POOL_PAIRS:
+                st_wgrp(q)
             w = PW * 4
             nc.vector.tensor_tensor(
                 out=wgrp[q][:, g * w:(g + 1) * w].rearrange("p (o u e) -> p o u e", u=2, e=2),
@@ -167,27 +200,27 @@ def tile_optimalnet_pb_kernel(tc, vi, W_bytes, W_scale, b, out_0, out_1):
             nc.vector.quantize_mx(out=wcod[q][:, c0:c1].bitcast(FP8X4), scales=wscl[q][:, c0:c1],
                                   in_=wgrp[q][:, 4 * c0:4 * c1])
 
-        def mx_passes(q, a, g0, g1):
+        def mx_passes(q, a, gs, first, last):
             j = 2 * q + a
-            if g0 == 0:
+            if first:
                 acc[j] = psa.tile([P, B], F32, name="acc", tag="acc")
-            for g in range(g0, g1):
+            for g in gs:
                 c0 = g * PW + a * P
                 nc.tensor.matmul_mx(out=acc[j][:], lhsT=wcod[q][:, c0:c0 + P].bitcast(FP8X4),
                                     lhsT_scale=wscl[q][:, c0:c0 + P],
                                     rhs=vi_cod[:, g * B:(g + 1) * B].bitcast(FP8X4),
-                                    rhs_scale=vi_scl[:, g * B:(g + 1) * B], start=(g == 0), stop=(g == G - 1))
-            if g1 == G:
+                                    rhs_scale=vi_scl[:, g * B:(g + 1) * B], start=(first and g == gs[0]), stop=(last and g == gs[-1]))
+            if last:
                 vjt[j] = vjp.tile([P, B], F32, name="vjt")
                 nc.scalar.activation(out=vjt[j][:], in_=acc[j][:], func=ACT.Relu, bias=b_col[:, j:j + 1], scale=1.0,
                                      accum_out=sums[:, j:j + 1])
 
         def st_mx(q):
             for a in range(2):
-                mx_passes(q, a, 0, G)
+                mx_passes(q, a, range(G), True, True)
 
         def st_back(q):
-            m_ps = psm.tile([P, PW], F32, name="m_ps", tag="sm")
+            m_ps = psx.tile([P, PW], F32, name="m_ps", tag="xt")
             for a in range(2):
                 j = 2 * q + a
                 nc.tensor.transpose(m_ps[:, a * P:(a + 1) * P], sums[:, j:j + 1].to_broadcast([P, P]), ident_f[:])
@@ -210,7 +243,7 @@ def tile_optimalnet_pb_kernel(tc, vi, W_bytes, W_scale, b, out_0, out_1):
 
         def last_back(a):
             j = 2 * (NQ - 1) + a
-            m_ps = psm.tile([P, PW], F32, name="m_ps", tag="sm")
+            m_ps = psx.tile([P, PW], F32, name="m_ps", tag="xt")
             nc.tensor.transpose(m_ps[:, 0:P], sums[:, j:j + 1].to_broadcast([P, P]), ident_f[:])
             nc.scalar.mul(out=m_all[:, j * P:(j + 1) * P], in_=m_ps[:, 0:P], mul=1.0 / B)
             ob[j] = pso.tile([P, NR, P], F32, name="ob", tag="ob")
@@ -232,47 +265,65 @@ def tile_optimalnet_pb_kernel(tc, vi, W_bytes, W_scale, b, out_0, out_1):
             if 0 <= i < NU:
                 fn(i // G, i % G)
 
-        def pair_at(i):
-            return i // G if i >= 0 and i % G == 0 and i // G < NQ - 1 else None
+        seq = [(0, g) for g in range(G)] + [(q, g) for q in range(1, NQ)
+                                            for g in ((3, 0, 1, 2) if q in POOL_PAIRS else (0, 1, 2, 3))]
+
+        def wt_seq(n):
+            if n < NU:
+                q, g = seq[n]
+                st_wt(q, g)
+                if q in POOL_PAIRS and g == G - 1:
+                    st_wgrp(q)
+                    st_pool(q, g)
 
         first_casts()
         for j in range(2, 6):
             st_cast(j)
         st_wt(0, 0)
         st_wt(0, 1)
-        for i in range(NU + 1):
-            run(st_prod, i)
-            if i % 2 == 0 and 0 <= i - 2 < NU - 2:
-                st_q((i - 2) // G, (i - 2) % G, (i - 2) % G + 2)
-            if i == 6:
+        st_wt(0, 2)
+        for i in range(NU + 2):
+            if i == NU - 2:
+                st_q(NQ - 1, 0, 2)
+                st_q(NQ - 1, 3, 4)
+            else:
+                run(st_prod, i)
+                if i % 2 == 0 and 0 <= i - 2 < NU - 2:
+                    st_q((i - 2) // G, (i - 2) % G, (i - 2) % G + 2)
+            if i == VQ:
                 vi_quant()
-            if pair_at(i - 10) is not None:
-                st_out(pair_at(i - 10))
+            for q in range(NQ - 1):
+                if out_step(q) == i:
+                    st_out(q)
+            if i == NU - 2:
+                run(st_prod, i)
+                st_q(NQ - 1, 2, 3)
             if i < NR:
                 vi_turn(i)
-            run(st_wt, i + 2)
-            if i == 0:
+            if i == 3:
                 b_turn()
+            wt_seq(i + 3)
             for j in range(6, NJ):
-                if i == 4 * (j // 2) - 6 + j % 2:
+                if i == max(4 * (j // 2) - CL + j % 2, 1):
                     st_cast(j)
-            if pair_at(i - 8) is not None:
-                st_back(pair_at(i - 8))
-            if 4 <= i < 4 + NR:
-                row_sum(i - 4)
-            if i == 7:
-                st_mx(0)
-            elif i >= 9 and pair_at(i - 5) is not None:
-                st_mx(pair_at(i - 5))
+            if i in RS:
+                row_sum(RS.index(i))
+            for q in range(NQ - 1):
+                if back_step(q) == i:
+                    st_back(q)
+            for q in range(NQ - 1):
+                if mx_step(q) == i:
+                    st_mx(q)
+            if i == NU - 2:
+                for a in range(2):
+                    mx_passes(NQ - 1, a, (3, 0, 1), True, False)
             if i == NU - 1:
                 for a in range(2):
-                    mx_passes(NQ - 1, a, 0, 2)
+                    mx_passes(NQ - 1, a, (2,), False, True)
 
-        st_q(NQ - 1, 2, 3)
-        st_q(NQ - 1, 3, 4)
-        for a in range(2):
-            mx_passes(NQ - 1, a, 2, G)
-        st_out(NQ - 2)
+        for q in range(NQ - 1):
+            if out_step(q) >= NU + 2:
+                st_out(q)
         for a in range(2):
             last_back(a)
             last_out(a)

@@ -23,7 +23,7 @@ NQ = NJ // 2
 PW = 2 * P
 NR = B // P
 
-VQ, OUT, BACK, MX, MX0, OUT0 = 6, 11, 7, 4, 6, 15
+VQ, OUT, BACK, MX, MX0, OUT0 = 6, 10, 7, 4, 6, 11
 
 
 def mx_step(q):
@@ -38,10 +38,10 @@ def out_step(q):
     return max(G * q + OUT, back_step(q) + 1, OUT0 + 2 * q)
 
 
-RS = (4, 5, 6, 7)
-POOL_CASTS = (2, 3, 4, 5, 6, 7, 8, 9, 10)
-POOL_PAIRS = (2, 3, 4, 5, 6, 7)
-CL = 9
+RS = (3, 4, 6, 8)
+POOL_CASTS = (2, 3, 4, 5, 6)
+POOL_PAIRS = ()
+CL = 6
 
 
 def tile_optimalnet_pb_kernel(tc, vi, W_bytes, W_scale, b, out_0, out_1):
@@ -283,9 +283,8 @@ def tile_optimalnet_pb_kernel(tc, vi, W_bytes, W_scale, b, out_0, out_1):
         st_wt(0, 1)
         st_wt(0, 2)
         for i in range(NU + 2):
-            if i == NU - 2:
-                st_q(NQ - 1, 0, 2)
-                st_q(NQ - 1, 3, 4)
+            if i == NU - 1:
+                st_q(NQ - 1, 2, 3)
             else:
                 run(st_prod, i)
                 if i % 2 == 0 and 0 <= i - 2 < NU - 2:
@@ -295,9 +294,9 @@ def tile_optimalnet_pb_kernel(tc, vi, W_bytes, W_scale, b, out_0, out_1):
             for q in range(NQ - 1):
                 if out_step(q) == i:
                     st_out(q)
-            if i == NU - 2:
+            if i == NU - 1:
                 run(st_prod, i)
-                st_q(NQ - 1, 2, 3)
+                st_q(NQ - 1, 3, 4)
             if i < NR:
                 vi_turn(i)
             if i == 3:
@@ -316,10 +315,10 @@ def tile_optimalnet_pb_kernel(tc, vi, W_bytes, W_scale, b, out_0, out_1):
                     st_mx(q)
             if i == NU - 2:
                 for a in range(2):
-                    mx_passes(NQ - 1, a, (3, 0, 1), True, False)
+                    mx_passes(NQ - 1, a, (0, 1), True, False)
             if i == NU - 1:
                 for a in range(2):
-                    mx_passes(NQ - 1, a, (2,), False, True)
+                    mx_passes(NQ - 1, a, (2, 3), False, True)
 
         for q in range(NQ - 1):
             if out_step(q) >= NU + 2:

@@ -23,25 +23,25 @@ NQ = NJ // 2
 PW = 2 * P
 NR = B // P
 
-VQ, OUT, BACK, MX, MX0, OUT0 = 6, 10, 7, 4, 6, 11
+RS = (3, 6, 10, 13)
+VQ = 6
+MX0 = 8
+A = 4
+BM = 7
+OB = 9
+Z = 11
+OUT0 = 15
+CL = 9
+POOL_CASTS = (2, 3, 4, 5, 6, 7, 8, 9, 10, 11, 12, 13)
+SG_PAIRS = (2, 3, 4, 5, 6, 7)
 
 
-def mx_step(q):
-    return max(G * q + MX, MX0)
+def mx_step(q, a):
+    return max(G * q + A, MX0 + 2 * q) + a
 
 
-def back_step(q):
-    return max(G * q + BACK, mx_step(q) + 1, OUT0 + 2 * q - 2)
-
-
-def out_step(q):
-    return max(G * q + OUT, back_step(q) + 1, OUT0 + 2 * q)
-
-
-RS = (3, 4, 6, 8)
-POOL_CASTS = (2, 3, 4, 5, 6)
-POOL_PAIRS = ()
-CL = 6
+def back_step(q, d):
+    return max(G * q + d, OUT0 + d - Z + 3 * q)
 
 
 def tile_optimalnet_pb_kernel(tc, vi, W_bytes, W_scale, b, out_0, out_1):
@@ -50,15 +50,16 @@ def tile_optimalnet_pb_kernel(tc, vi, W_bytes, W_scale, b, out_0, out_1):
         const = ctx.enter_context(tc.tile_pool(name="const", bufs=1))
         wbp = ctx.enter_context(tc.tile_pool(name="wbp", bufs=1))
         wkp = ctx.enter_context(tc.tile_pool(name="wkp", bufs=NJ))
-        wip = ctx.enter_context(tc.tile_pool(name="wip", bufs=2))
+        plp = ctx.enter_context(tc.tile_pool(name="plp", bufs=2))
         wgp = ctx.enter_context(tc.tile_pool(name="wgp", bufs=3))
         wcp = ctx.enter_context(tc.tile_pool(name="wcp", bufs=3))
         vjp = ctx.enter_context(tc.tile_pool(name="vjp", bufs=6))
-        osp = ctx.enter_context(tc.tile_pool(name="osp", bufs=4))
+        osp = ctx.enter_context(tc.tile_pool(name="osp", bufs=6))
         psx = ctx.enter_context(tc.psum_pool(name="psx", bufs=4))
         psa = ctx.enter_context(tc.psum_pool(name="psa", bufs=2))
         pso = ctx.enter_context(tc.psum_pool(name="pso", bufs=2))
-        ctx.enter_context(tc.manual_schedule(engines={mybir.EngineType.PE, mybir.EngineType.Activation, mybir.EngineType.DVE}))
+        ctx.enter_context(tc.manual_schedule(engines={mybir.EngineType.PE, mybir.EngineType.Activation, mybir.EngineType.DVE,
+                                                    mybir.EngineType.Pool}))
 
         s_t = const.tile([P, G, 4], F32, name="s_t")
         nc.scalar.dma_start(out=s_t[:], in_=W_scale.rearrange("o (g p t) -> p (o g) t", p=P, t=4))
@@ -133,7 +134,7 @@ def tile_optimalnet_pb_kernel(tc, vi, W_bytes, W_scale, b, out_0, out_1):
         def row_sum(rt):
             nc.scalar.activation(out=junk[:], in_=vi_sb[rt][:], func=ACT.Copy, scale=C, accum_out=rsc[:, rt:rt + 1])
 
-        sums = const.tile([P, NJ], F32, name="sums")
+        sums = const.tile([P, NJ, 1], F32, name="sums")
         m_all = const.tile([P, O], F32, name="m_all")
         wk = {}
         xt = {}
@@ -168,23 +169,22 @@ def tile_optimalnet_pb_kernel(tc, vi, W_bytes, W_scale, b, out_0, out_1):
                     nc.tensor.transpose(xt[q, g][:, u, a * P:(a + 1) * P], words[:, 256 * g + u:256 * (g + 1):2],
                                         ident_f[:])
 
-        def st_wgrp(q):
+        def sg_prod(q, g):
             wgrp[q] = wgp.tile([P, G * PW * 4], BF16, name="wgrp", align_bytes=64)
-
-        def st_pool(q, g):
+            planes = plp.tile([P, 4, PW], BF16, name="planes")
+            halves = xt[q, g][:].bitcast(BF16).rearrange("p u (o e) -> p u e o", e=2)
+            for t in range(4):
+                nc.scalar.activation(out=planes[:, t, :], in_=halves[:, t // 2, t % 2, :], func=ACT.Copy,
+                                     scale=s_t[:, g, t:t + 1])
             w = PW * 4
-            wint = wip.tile([P, w], BF16, name="wint", align_bytes=64)
-            nc.scalar.copy(out=wint[:].bitcast(F32).rearrange("p (o u) -> p o u", u=2),
-                           in_=xt[q, g][:].rearrange("p u o -> p o u"))
-            nc.gpsimd.tensor_tensor(out=wgrp[q][:, g * w:(g + 1) * w].rearrange("p (o t) -> p o t", t=4),
-                                    in0=wint[:].rearrange("p (o t) -> p o t", t=4),
-                                    in1=s_t[:, g:g + 1, :].to_broadcast([P, PW, 4]), op=ALU.mult)
+            nc.gpsimd.tensor_copy(out=wgrp[q][:, g * w:(g + 1) * w].rearrange("p (o t) -> p o t", t=4),
+                                  in_=planes[:].rearrange("p t o -> p o t"))
 
         def st_prod(q, g):
-            if q in POOL_PAIRS and g == G - 1:
+            if q in SG_PAIRS and g == G - 1:
                 return
-            if g == 0 and q not in POOL_PAIRS:
-                st_wgrp(q)
+            if q not in SG_PAIRS and g == 0:
+                wgrp[q] = wgp.tile([P, G * PW * 4], BF16, name="wgrp", align_bytes=64)
             w = PW * 4
             nc.vector.tensor_tensor(
                 out=wgrp[q][:, g * w:(g + 1) * w].rearrange("p (o u e) -> p o u e", u=2, e=2),
@@ -213,38 +213,37 @@ def tile_optimalnet_pb_kernel(tc, vi, W_bytes, W_scale, b, out_0, out_1):
             if last:
                 vjt[j] = vjp.tile([P, B], F32, name="vjt")
                 nc.scalar.activation(out=vjt[j][:], in_=acc[j][:], func=ACT.Relu, bias=b_col[:, j:j + 1], scale=1.0,
-                                     accum_out=sums[:, j:j + 1])
+                                     accum_out=sums[:, j, :])
 
-        def st_mx(q):
-            for a in range(2):
-                mx_passes(q, a, range(G), True, True)
 
-        def st_back(q):
+        def st_back_m(q):
             m_ps = psx.tile([P, PW], F32, name="m_ps", tag="xt")
             for a in range(2):
                 j = 2 * q + a
-                nc.tensor.transpose(m_ps[:, a * P:(a + 1) * P], sums[:, j:j + 1].to_broadcast([P, P]), ident_f[:])
-            for rp in range(2):
-                ob[q, rp] = pso.tile([P, 2, PW], F32, name="ob", tag="ob")
-                for rl in range(2):
-                    rt = 2 * rp + rl
-                    for a in range(2):
-                        nc.tensor.transpose(ob[q, rp][:, rl, a * P:(a + 1) * P],
-                                            vjt[2 * q + a][:, rt * P:(rt + 1) * P], ident_f[:])
+                nc.tensor.transpose(m_ps[:, a * P:(a + 1) * P], sums[:, j, :].to_broadcast([P, P]), ident_f[:])
             nc.scalar.mul(out=m_all[:, q * PW:(q + 1) * PW], in_=m_ps[:], mul=1.0 / B)
 
-        def st_out(q):
-            osb = osp.tile([P, NR, PW], F32, name="osb")
-            for rt in range(NR):
-                nc.vector.scalar_tensor_tensor(out=osb[:, rt, :], in0=m_all[:, q * PW:(q + 1) * PW],
-                                               scalar=rsc[:, rt:rt + 1], in1=ob[q, rt // 2][:, rt % 2, :],
+        def st_back(q, rp):
+            ob[q, rp] = pso.tile([P, 2, PW], F32, name="ob", tag="ob")
+            for rl in range(2):
+                rt = 2 * rp + rl
+                for a in range(2):
+                    nc.tensor.transpose(ob[q, rp][:, rl, a * P:(a + 1) * P],
+                                        vjt[2 * q + a][:, rt * P:(rt + 1) * P], ident_f[:])
+
+        def st_out(q, rp):
+            osb = osp.tile([P, 2, PW], F32, name="osb")
+            for rl in range(2):
+                rt = 2 * rp + rl
+                nc.vector.scalar_tensor_tensor(out=osb[:, rl, :], in0=m_all[:, q * PW:(q + 1) * PW],
+                                               scalar=rsc[:, rt:rt + 1], in1=ob[q, rp][:, rl, :],
                                                op0=ALU.mult, op1=ALU.add)
-            nc.sync.dma_start(out=out_v[:, :, q * PW:(q + 1) * PW], in_=osb[:])
+            nc.sync.dma_start(out=out_v[:, 2 * rp:2 * rp + 2, q * PW:(q + 1) * PW], in_=osb[:])
 
         def last_back(a):
             j = 2 * (NQ - 1) + a
             m_ps = psx.tile([P, PW], F32, name="m_ps", tag="xt")
-            nc.tensor.transpose(m_ps[:, 0:P], sums[:, j:j + 1].to_broadcast([P, P]), ident_f[:])
+            nc.tensor.transpose(m_ps[:, 0:P], sums[:, j, :].to_broadcast([P, P]), ident_f[:])
             nc.scalar.mul(out=m_all[:, j * P:(j + 1) * P], in_=m_ps[:, 0:P], mul=1.0 / B)
             ob[j] = pso.tile([P, NR, P], F32, name="ob", tag="ob")
             for rt in range(NR):
@@ -265,16 +264,14 @@ def tile_optimalnet_pb_kernel(tc, vi, W_bytes, W_scale, b, out_0, out_1):
             if 0 <= i < NU:
                 fn(i // G, i % G)
 
-        seq = [(0, g) for g in range(G)] + [(q, g) for q in range(1, NQ)
-                                            for g in ((3, 0, 1, 2) if q in POOL_PAIRS else (0, 1, 2, 3))]
+        seq = [(q, g) for q in range(NQ) for g in ((3, 0, 1, 2) if q in SG_PAIRS else (0, 1, 2, 3))]
 
         def wt_seq(n):
             if n < NU:
                 q, g = seq[n]
                 st_wt(q, g)
-                if q in POOL_PAIRS and g == G - 1:
-                    st_wgrp(q)
-                    st_pool(q, g)
+                if q in SG_PAIRS and g == G - 1:
+                    sg_prod(q, g)
 
         first_casts()
         for j in range(2, 6):
@@ -282,9 +279,10 @@ def tile_optimalnet_pb_kernel(tc, vi, W_bytes, W_scale, b, out_0, out_1):
         st_wt(0, 0)
         st_wt(0, 1)
         st_wt(0, 2)
-        for i in range(NU + 2):
-            if i == NU - 1:
-                st_q(NQ - 1, 2, 3)
+        for i in range(NU + 8):
+            if i == NU - 2:
+                st_q(NQ - 1, 0, 2)
+                st_q(NQ - 1, 3, 4)
             else:
                 run(st_prod, i)
                 if i % 2 == 0 and 0 <= i - 2 < NU - 2:
@@ -292,11 +290,12 @@ def tile_optimalnet_pb_kernel(tc, vi, W_bytes, W_scale, b, out_0, out_1):
             if i == VQ:
                 vi_quant()
             for q in range(NQ - 1):
-                if out_step(q) == i:
-                    st_out(q)
-            if i == NU - 1:
+                for rp in range(2):
+                    if back_step(q, Z) + rp == i:
+                        st_out(q, rp)
+            if i == NU - 2:
                 run(st_prod, i)
-                st_q(NQ - 1, 3, 4)
+                st_q(NQ - 1, 2, 3)
             if i < NR:
                 vi_turn(i)
             if i == 3:
@@ -308,21 +307,22 @@ def tile_optimalnet_pb_kernel(tc, vi, W_bytes, W_scale, b, out_0, out_1):
             if i in RS:
                 row_sum(RS.index(i))
             for q in range(NQ - 1):
-                if back_step(q) == i:
-                    st_back(q)
+                for rp in range(2):
+                    if back_step(q, OB) + rp == i:
+                        st_back(q, rp)
+                if back_step(q, BM) == i:
+                    st_back_m(q)
             for q in range(NQ - 1):
-                if mx_step(q) == i:
-                    st_mx(q)
+                for a in range(2):
+                    if mx_step(q, a) == i:
+                        mx_passes(q, a, range(G), True, True)
             if i == NU - 2:
                 for a in range(2):
-                    mx_passes(NQ - 1, a, (0, 1), True, False)
+                    mx_passes(NQ - 1, a, (3, 0, 1), True, False)
             if i == NU - 1:
                 for a in range(2):
-                    mx_passes(NQ - 1, a, (2, 3), False, True)
+                    mx_passes(NQ - 1, a, (2,), False, True)
 
-        for q in range(NQ - 1):
-            if out_step(q) >= NU + 2:
-                st_out(q)
         for a in range(2):
             last_back(a)
             last_out(a)

@@ -23,21 +23,25 @@ NQ = NJ // 2
 PW = 2 * P
 NR = B // P
 
-RS = (3, 6, 10, 13)
-VQ = 6
+RS = (2, 6, 8, 10)
+VQ = 7
 MX0 = 8
-A = 4
-BM = 7
-OB = 9
-Z = 11
-OUT0 = 15
-CL = 9
-POOL_CASTS = (2, 3, 4, 5, 6, 7, 8, 9, 10, 11, 12, 13)
-SG_PAIRS = (2, 3, 4, 5, 6, 7)
+A = 6
+BM = 9
+OB = 13
+Z = 14
+OUT0 = 14
+CL = 8
+POOL_CASTS = (2, 3, 4, 5, 6)
+SG_PAIRS = (3, 4, 5, 6, 7)
 
 
-def mx_step(q, a):
-    return max(G * q + A, MX0 + 2 * q) + a
+MXG = ((0,), (1,), (2,), (3,), (4,), (5,), (6,))
+
+
+def mx_step(q):
+    last = [grp for grp in MXG if q in grp][0][-1]
+    return max(G * last + A, MX0 + 2 * q)
 
 
 def back_step(q, d):
@@ -313,8 +317,8 @@ def tile_optimalnet_pb_kernel(tc, vi, W_bytes, W_scale, b, out_0, out_1):
                 if back_step(q, BM) == i:
                     st_back_m(q)
             for q in range(NQ - 1):
-                for a in range(2):
-                    if mx_step(q, a) == i:
+                if mx_step(q) == i:
+                    for a in range(2):
                         mx_passes(q, a, range(G), True, True)
             if i == NU - 2:
                 for a in range(2):

from contextlib import ExitStack

import concourse.mybir as mybir
from concourse.masks import make_identity

F32 = mybir.dt.float32
BF16 = mybir.dt.bfloat16
U32 = mybir.dt.uint32
U8 = mybir.dt.uint8
FP8 = mybir.dt.float8_e4m3fn
FP8X4 = mybir.dt.float8_e4m3fn_x4
ACT = mybir.ActivationFunctionType
ALU = mybir.AluOpType

B, K, O = 512, 2048, 2048
C = 0.01 * 0.001 / 1
FLOPS = 2 * B * K * O

P = 128
G = K // 512
NJ = O // P
NQ = NJ // 2
PW = 2 * P
NR = B // P

RS = (2, 6, 8, 10)
VQ = 7
MX0 = 8
A = 6
BM = 9
OB = 13
Z = 14
OUT0 = 14
CL = 8
POOL_CASTS = (2, 3, 4, 5, 6)
SG_PAIRS = (3, 4, 5, 6, 7)


MXG = ((0,), (1,), (2,), (3,), (4,), (5,), (6,))


def mx_step(q):
    last = [grp for grp in MXG if q in grp][0][-1]
    return max(G * last + A, MX0 + 2 * q)


def back_step(q, d):
    return max(G * q + d, OUT0 + d - Z + 3 * q)


def tile_optimalnet_pb_kernel(tc, vi, W_bytes, W_scale, b, out_0, out_1):
    nc = tc.nc
    with ExitStack() as ctx:
        const = ctx.enter_context(tc.tile_pool(name="const", bufs=1))
        wbp = ctx.enter_context(tc.tile_pool(name="wbp", bufs=1))
        wkp = ctx.enter_context(tc.tile_pool(name="wkp", bufs=NJ))
        plp = ctx.enter_context(tc.tile_pool(name="plp", bufs=2))
        wgp = ctx.enter_context(tc.tile_pool(name="wgp", bufs=3))
        wcp = ctx.enter_context(tc.tile_pool(name="wcp", bufs=3))
        vjp = ctx.enter_context(tc.tile_pool(name="vjp", bufs=6))
        osp = ctx.enter_context(tc.tile_pool(name="osp", bufs=6))
        psx = ctx.enter_context(tc.psum_pool(name="psx", bufs=4))
        psa = ctx.enter_context(tc.psum_pool(name="psa", bufs=2))
        pso = ctx.enter_context(tc.psum_pool(name="pso", bufs=2))
        ctx.enter_context(tc.manual_schedule(engines={mybir.EngineType.PE, mybir.EngineType.Activation, mybir.EngineType.DVE,
                                                    mybir.EngineType.Pool}))

        s_t = const.tile([P, G, 4], F32, name="s_t")
        nc.scalar.dma_start(out=s_t[:], in_=W_scale.rearrange("o (g p t) -> p (o g) t", p=P, t=4))

        ident_f = const.tile([P, P], F32, name="ident_f")
        make_identity(nc, ident_f[:])
        ident_b = const.tile([P, P], BF16, name="ident_b")
        make_identity(nc, ident_b[:])
        warm = const.tile([P, 1], F32, name="warm")
        nc.vector.memset(warm[:], 0.0)
        warm2 = const.tile([P, 1], F32, name="warm2")
        nc.scalar.activation(out=warm2[:], in_=warm[:], func=ACT.Relu)
        b_rows = const.tile([P, P], BF16, name="b_rows")
        nc.gpsimd.memset(b_rows[:], 0.0)

        wb = {}
        vi_sb = {}

        def load_w(j):
            wb[j] = wbp.tile([P, K], U8, name="wb%d" % j)
            nc.sync.dma_start(out=wb[j][:], in_=W_bytes[j * P:(j + 1) * P, :])

        def load_vi(rt):
            vi_sb[rt] = const.tile([P, K], BF16, name="vi_sb%d" % rt)
            nc.sync.dma_start(out=vi_sb[rt][:], in_=vi[rt * P:(rt + 1) * P, :])

        load_w(0)
        load_w(1)
        load_w(2)
        load_vi(0)
        nc.sync.dma_start(out=b_rows[0:NJ, :], in_=b.rearrange("(j p) -> j p", p=P))
        load_w(3)
        load_vi(1)
        load_vi(2)
        load_vi(3)
        for j in range(4, NJ):
            load_w(j)

        vi_grp = const.tile([P, G * B * 4], BF16, name="vi_grp", align_bytes=64)
        vi_grp_w = vi_grp[:].bitcast(F32).rearrange("p (g r u) -> p g r u", g=G, u=2)
        vi_cod = const.tile([P, G * B], U32, name="vi_cod", align_bytes=64)
        vi_scl = const.tile([P, G * B], U8, name="vi_scl", align_bytes=64)

        def vi_turn(rt):
            words = vi_sb[rt][:].bitcast(F32)
            pool, tag = ((psa, "acc"), (pso, "ob"))[rt % 2]
            for gp in range(2):
                xv = pool.tile([P, 2, 2, P], F32, name="xv", tag=tag)
                for gl in range(2):
                    g = 2 * gp + gl
                    for u in range(2):
                        nc.tensor.transpose(xv[:, gl, u, :], words[:, 256 * g + u:256 * (g + 1):2], ident_f[:])
                nc.scalar.copy(out=vi_grp_w[:, 2 * gp:2 * gp + 2, rt * P:(rt + 1) * P, :],
                               in_=xv[:].rearrange("p g u r -> p g r u"))

        def vi_quant():
            for g in range(G):
                c0 = g * B
                nc.vector.quantize_mx(out=vi_cod[:, c0:c0 + B].bitcast(FP8X4), scales=vi_scl[:, c0:c0 + B],
                                      in_=vi_grp[:, 4 * c0:4 * (c0 + B)])

        b_col = const.tile([P, NJ], F32, name="b_col")

        def b_turn():
            b_ps = psx.tile([P, P], BF16, name="b_ps", tag="xt")
            nc.tensor.transpose(b_ps[:], b_rows[:], ident_b[:])
            nc.scalar.copy(out=b_col[:], in_=b_ps[:, 0:NJ])

        rsc = const.tile([P, NR], F32, name="rsc")
        junk = const.tile([P, K], BF16, name="junk")

        def row_sum(rt):
            nc.scalar.activation(out=junk[:], in_=vi_sb[rt][:], func=ACT.Copy, scale=C, accum_out=rsc[:, rt:rt + 1])

        sums = const.tile([P, NJ, 1], F32, name="sums")
        m_all = const.tile([P, O], F32, name="m_all")
        wk = {}
        xt = {}
        wgrp = {}
        wcod = {}
        wscl = {}
        acc = {}
        vjt = {}
        ob = {}
        out_v = out_0.rearrange("(t p) o -> p t o", p=P)

        def cast(fn, j, k0, k1):
            fn(out=wk[j][:, k0:k1], in_=wb[j][:, k0:k1].bitcast(FP8))

        def st_cast(j):
            wk[j] = wkp.tile([P, K], BF16, name="wk")
            cast(nc.gpsimd.tensor_copy if j in POOL_CASTS else nc.scalar.copy, j, 0, K)

        def first_casts():
            for j in range(2):
                wk[j] = wkp.tile([P, K], BF16, name="wk")
            cast(nc.vector.tensor_copy, 0, 0, 512)
            cast(nc.vector.tensor_copy, 1, 0, 512)
            cast(nc.scalar.copy, 1, 512, K)
            cast(nc.vector.tensor_copy, 0, 512, K)

        def st_wt(q, g):
            xt[q, g] = psx.tile([P, 2, PW], F32, name="xt", tag="xt")
            for a in range(2):
                words = wk[2 * q + a][:].bitcast(F32)
                for u in range(2):
                    nc.tensor.transpose(xt[q, g][:, u, a * P:(a + 1) * P], words[:, 256 * g + u:256 * (g + 1):2],
                                        ident_f[:])

        def sg_prod(q, g):
            wgrp[q] = wgp.tile([P, G * PW * 4], BF16, name="wgrp", align_bytes=64)
            planes = plp.tile([P, 4, PW], BF16, name="planes")
            halves = xt[q, g][:].bitcast(BF16).rearrange("p u (o e) -> p u e o", e=2)
            for t in range(4):
                nc.scalar.activation(out=planes[:, t, :], in_=halves[:, t // 2, t % 2, :], func=ACT.Copy,
                                     scale=s_t[:, g, t:t + 1])
            w = PW * 4
            nc.gpsimd.tensor_copy(out=wgrp[q][:, g * w:(g + 1) * w].rearrange("p (o t) -> p o t", t=4),
                                  in_=planes[:].rearrange("p t o -> p o t"))

        def st_prod(q, g):
            if q in SG_PAIRS and g == G - 1:
                return
            if q not in SG_PAIRS and g == 0:
                wgrp[q] = wgp.tile([P, G * PW * 4], BF16, name="wgrp", align_bytes=64)
            w = PW * 4
            nc.vector.tensor_tensor(
                out=wgrp[q][:, g * w:(g + 1) * w].rearrange("p (o u e) -> p o u e", u=2, e=2),
                in0=xt[q, g][:].bitcast(BF16).rearrange("p u (o e) -> p o u e", e=2),
                in1=s_t[:, g:g + 1, :].rearrange("p o (u e) -> p o u e", u=2).to_broadcast([P, PW, 2, 2]),
                op=ALU.mult)

        def st_q(q, g0, g1):
            if g0 == 0:
                wcod[q] = wcp.tile([P, G * PW], U32, name="wcod", align_bytes=64)
                wscl[q] = wcp.tile([P, G * PW], U8, name="wscl", align_bytes=64)
            c0, c1 = g0 * PW, g1 * PW
            nc.vector.quantize_mx(out=wcod[q][:, c0:c1].bitcast(FP8X4), scales=wscl[q][:, c0:c1],
                                  in_=wgrp[q][:, 4 * c0:4 * c1])

        def mx_passes(q, a, gs, first, last):
            j = 2 * q + a
            if first:
                acc[j] = psa.tile([P, B], F32, name="acc", tag="acc")
            for g in gs:
                c0 = g * PW + a * P
                nc.tensor.matmul_mx(out=acc[j][:], lhsT=wcod[q][:, c0:c0 + P].bitcast(FP8X4),
                                    lhsT_scale=wscl[q][:, c0:c0 + P],
                                    rhs=vi_cod[:, g * B:(g + 1) * B].bitcast(FP8X4),
                                    rhs_scale=vi_scl[:, g * B:(g + 1) * B], start=(first and g == gs[0]), stop=(last and g == gs[-1]))
            if last:
                vjt[j] = vjp.tile([P, B], F32, name="vjt")
                nc.scalar.activation(out=vjt[j][:], in_=acc[j][:], func=ACT.Relu, bias=b_col[:, j:j + 1], scale=1.0,
                                     accum_out=sums[:, j, :])


        def st_back_m(q):
            m_ps = psx.tile([P, PW], F32, name="m_ps", tag="xt")
            for a in range(2):
                j = 2 * q + a
                nc.tensor.transpose(m_ps[:, a * P:(a + 1) * P], sums[:, j, :].to_broadcast([P, P]), ident_f[:])
            nc.scalar.mul(out=m_all[:, q * PW:(q + 1) * PW], in_=m_ps[:], mul=1.0 / B)

        def st_back(q, rp):
            ob[q, rp] = pso.tile([P, 2, PW], F32, name="ob", tag="ob")
            for rl in range(2):
                rt = 2 * rp + rl
                for a in range(2):
                    nc.tensor.transpose(ob[q, rp][:, rl, a * P:(a + 1) * P],
                                        vjt[2 * q + a][:, rt * P:(rt + 1) * P], ident_f[:])

        def st_out(q, rp):
            osb = osp.tile([P, 2, PW], F32, name="osb")
            for rl in range(2):
                rt = 2 * rp + rl
                nc.vector.scalar_tensor_tensor(out=osb[:, rl, :], in0=m_all[:, q * PW:(q + 1) * PW],
                                               scalar=rsc[:, rt:rt + 1], in1=ob[q, rp][:, rl, :],
                                               op0=ALU.mult, op1=ALU.add)
            nc.sync.dma_start(out=out_v[:, 2 * rp:2 * rp + 2, q * PW:(q + 1) * PW], in_=osb[:])

        def last_back(a):
            j = 2 * (NQ - 1) + a
            m_ps = psx.tile([P, PW], F32, name="m_ps", tag="xt")
            nc.tensor.transpose(m_ps[:, 0:P], sums[:, j, :].to_broadcast([P, P]), ident_f[:])
            nc.scalar.mul(out=m_all[:, j * P:(j + 1) * P], in_=m_ps[:, 0:P], mul=1.0 / B)
            ob[j] = pso.tile([P, NR, P], F32, name="ob", tag="ob")
            for rt in range(NR):
                nc.tensor.transpose(ob[j][:, rt, :], vjt[j][:, rt * P:(rt + 1) * P], ident_f[:])

        def last_out(a):
            j = 2 * (NQ - 1) + a
            osb = osp.tile([P, NR, P], F32, name="osb_l")
            for rt in range(NR):
                nc.vector.scalar_tensor_tensor(out=osb[:, rt, :], in0=m_all[:, j * P:(j + 1) * P],
                                               scalar=rsc[:, rt:rt + 1], in1=ob[j][:, rt, :],
                                               op0=ALU.mult, op1=ALU.add)
            nc.sync.dma_start(out=out_v[:, :, j * P:(j + 1) * P], in_=osb[:])

        NU = NQ * G

        def run(fn, i):
            if 0 <= i < NU:
                fn(i // G, i % G)

        seq = [(q, g) for q in range(NQ) for g in ((3, 0, 1, 2) if q in SG_PAIRS else (0, 1, 2, 3))]

        def wt_seq(n):
            if n < NU:
                q, g = seq[n]
                st_wt(q, g)
                if q in SG_PAIRS and g == G - 1:
                    sg_prod(q, g)

        first_casts()
        for j in range(2, 6):
            st_cast(j)
        st_wt(0, 0)
        st_wt(0, 1)
        st_wt(0, 2)
        for i in range(NU + 8):
            if i == NU - 2:
                st_q(NQ - 1, 0, 2)
                st_q(NQ - 1, 3, 4)
            else:
                run(st_prod, i)
                if i % 2 == 0 and 0 <= i - 2 < NU - 2:
                    st_q((i - 2) // G, (i - 2) % G, (i - 2) % G + 2)
            if i == VQ:
                vi_quant()
            for q in range(NQ - 1):
                for rp in range(2):
                    if back_step(q, Z) + rp == i:
                        st_out(q, rp)
            if i == NU - 2:
                run(st_prod, i)
                st_q(NQ - 1, 2, 3)
            if i < NR:
                vi_turn(i)
            if i == 3:
                b_turn()
            wt_seq(i + 3)
            for j in range(6, NJ):
                if i == max(4 * (j // 2) - CL + j % 2, 1):
                    st_cast(j)
            if i in RS:
                row_sum(RS.index(i))
            for q in range(NQ - 1):
                for rp in range(2):
                    if back_step(q, OB) + rp == i:
                        st_back(q, rp)
                if back_step(q, BM) == i:
                    st_back_m(q)
            for q in range(NQ - 1):
                if mx_step(q) == i:
                    for a in range(2):
                        mx_passes(q, a, range(G), True, True)
            if i == NU - 2:
                for a in range(2):
                    mx_passes(NQ - 1, a, (3, 0, 1), True, False)
            if i == NU - 1:
                for a in range(2):
                    mx_passes(NQ - 1, a, (2,), False, True)

        for a in range(2):
            last_back(a)
            last_out(a)
        nc.sync.dma_start(out=out_1.rearrange("(a o) -> a o", a=1), in_=m_all[0:1, :])
